import numpy as np
import ml_dtypes


def mxq(x, axis, fmt="e4m3"):
    dtype, down = {"e4m3": (ml_dtypes.float8_e4m3fn, 7), "e5m2": (ml_dtypes.float8_e5m2, 14)}[fmt]
    v = np.moveaxis(np.asarray(x, np.float32).astype(ml_dtypes.bfloat16).astype(np.float64), axis, -1)
    blocks = v.reshape(v.shape[:-1] + (-1, 32))
    amax = np.abs(blocks).max(-1, keepdims=True)
    byte = np.maximum(np.where(amax > 0, np.frexp(amax)[1] - 1 + 127, 0) - down, 1)
    scale = np.exp2(byte - 127.0)
    codes = (blocks / scale).astype(np.float32).astype(dtype).astype(np.float64)
    return np.moveaxis((codes * scale).reshape(v.shape), -1, axis)


WIDE = False


def mx_kscale(k):
    if not WIDE:
        return np.ones(k)
    levels = np.array([10, -10, 5, -5, 0])
    a = np.random.permutation(np.resize(levels, k // 512 * 4)).reshape(k // 512, 4)
    idx = np.arange(k)
    return np.exp2(a[idx // 512, idx % 128 // 32])


BF16 = ml_dtypes.bfloat16


def bf(x):
    return np.asarray(x, np.float32).astype(BF16)


def f64(x):
    return np.asarray(x).astype(np.float64)


B, L, S, D, H = 12, 384, 128, 512, 4
HD = D // H
T = S + L


def to_mha(t):
    return t.reshape(t.shape[0], t.shape[1], H, HD).transpose(0, 2, 1, 3)


def setup_inputs():
    s = mx_kscale(D)
    return {
        "q_rot": bf(np.random.standard_normal((B, H, T, HD))),
        "k_rot": bf(np.random.standard_normal((B, H, T, HD))),
        "x": bf(np.random.standard_normal((B, L, D)) * s),
        "c": bf(np.random.standard_normal((B, S, D)) * s),
        "Wv_x": bf(np.random.standard_normal((D, D)) * 3.0 / np.sqrt(D) / s[:, None]),
        "bv_x": bf(np.random.standard_normal(D) * 0.2),
        "Wv_c": bf(np.random.standard_normal((D, D)) * 3.0 / np.sqrt(D) / s[:, None]),
        "bv_c": bf(np.random.standard_normal(D) * 0.2),
    }


def reference(q_rot, k_rot, x, c, Wv_x, bv_x, Wv_c, bv_c):
    vc = to_mha((mxq(f64(c), 2, "e4m3") @ mxq(f64(Wv_c), 0, "e4m3")) + f64(bv_c))
    vx = to_mha((mxq(f64(x), 2, "e4m3") @ mxq(f64(Wv_x), 0, "e4m3")) + f64(bv_x))
    v = np.concatenate([vc, vx], axis=2)
    scores = f64(q_rot) @ f64(k_rot).transpose(0, 1, 3, 2) / np.sqrt(HD)
    e = np.exp(scores - scores.max(-1, keepdims=True))
    y = (mxq(e, 3, "e4m3") @ mxq(v, 2, "e4m3")) / e.sum(-1, keepdims=True)
    y = y.transpose(0, 2, 1, 3).reshape(B, T, D)
    return y[:, S:], y[:, :S]

@@ -1,0 +1,207 @@
+import math
+from contextlib import ExitStack
+
+import concourse.mybir as mybir
+from concourse.masks import make_identity
+
+BF16 = mybir.dt.bfloat16
+F32 = mybir.dt.float32
+U32 = mybir.dt.uint32
+U8 = mybir.dt.uint8
+FP8X4 = mybir.dt.float8_e4m3fn_x4
+ALU = mybir.AluOpType
+ACT = mybir.ActivationFunctionType
+
+B = 12
+H = 4
+T = 512
+D = 512
+HD = 128
+P = 128
+PACK = 4
+TILES = T // P
+HALF = 2 * P
+SCALE = 1.0 / math.sqrt(HD)
+
+FLOPS = 2 * B * T * D * D + 2 * 2 * B * H * T * T * HD
+
+
+def tile_dualstreamattentionwithrotaryembedding_pb_t_kernel(
+    tc, q_rot, k_rot, x, c, Wv_x, bv_x, Wv_c, bv_c, out_0, out_1
+):
+    nc = tc.nc
+    with ExitStack() as ctx:
+        const = ctx.enter_context(tc.tile_pool(name="const", bufs=1))
+        loads = ctx.enter_context(tc.tile_pool(name="loads", bufs=3))
+        batch = ctx.enter_context(tc.tile_pool(name="batch", bufs=2))
+        head = ctx.enter_context(tc.tile_pool(name="head", bufs=3))
+        rows = ctx.enter_context(tc.tile_pool(name="rows", bufs=6))
+        ps_scores = ctx.enter_context(tc.psum_pool(name="ps_scores", bufs=3))
+        ps_eT = ctx.enter_context(tc.psum_pool(name="ps_eT", bufs=2))
+        ps_y = ctx.enter_context(tc.psum_pool(name="ps_y", bufs=1))
+        ps_misc = ctx.enter_context(tc.psum_pool(name="ps_misc", bufs=2))
+
+        ident_bf16 = const.tile([P, P], BF16)
+        make_identity(nc, ident_bf16[:])
+        ident_f32 = const.tile([P, P], F32)
+        make_identity(nc, ident_f32[:])
+
+        w_codes = const.tile([P, 2, D], U32, align_bytes=64)
+        w_scales = const.tile([P, 2, D], U8, align_bytes=64)
+        for stream, w in enumerate((Wv_c, Wv_x)):
+            w_rows = const.tile([P, PACK * D], BF16, name="w_rows%d" % stream)
+            nc.sync.dma_start(
+                out=w_rows[:].rearrange("p (u m) -> p u m", u=2),
+                in_=w.rearrange("(u p e) n -> p u (e n)", u=2, e=2),
+            )
+            w_grouped = const.tile([P, D * PACK], BF16, name="w_grouped%d" % stream, align_bytes=64)
+            nc.vector.tensor_copy(
+                out=w_grouped[:].rearrange("p (n t) -> p n t", t=PACK),
+                in_=w_rows[:].rearrange("p (t n) -> p n t", t=PACK),
+            )
+            nc.vector.quantize_mx(
+                out=w_codes[:, stream, :].bitcast(FP8X4), scales=w_scales[:, stream, :], in_=w_grouped[:]
+            )
+
+        bias_rows = const.tile([P, 2, D], BF16)
+        nc.sync.dma_start(out=bias_rows[:, 0, :], in_=bv_c.partition_broadcast(P))
+        nc.sync.dma_start(out=bias_rows[:, 1, :], in_=bv_x.partition_broadcast(P))
+        bias_grouped = const.tile([P, D, PACK], F32)
+        nc.scalar.copy(out=bias_grouped[:], in_=bias_rows[:, 1, :].unsqueeze(2).to_broadcast([P, D, PACK]))
+        nc.scalar.copy(out=bias_grouped[:, :, 0], in_=bias_rows[:, 0, :])
+
+        for b in range(B):
+            xc_sb = loads.tile([P, TILES * D], BF16)
+            nc.sync.dma_start(out=xc_sb[:, 0:D], in_=c[b])
+            nc.sync.dma_start(
+                out=xc_sb[:, D:].rearrange("p (t k) -> p t k", k=D),
+                in_=x[b].rearrange("(t p) k -> p t k", p=P),
+            )
+            q_sb = loads.tile([P, H * TILES, HD], BF16)
+            nc.sync.dma_start(out=q_sb[:], in_=q_rot[b].rearrange("h (t p) d -> p (h t) d", p=P))
+            k_sb = loads.tile([P, H * TILES, HD], BF16)
+            nc.sync.dma_start(out=k_sb[:], in_=k_rot[b].rearrange("h (t p) d -> p (h t) d", p=P))
+
+            xc_words = xc_sb[:].bitcast(F32)
+            x_grouped = batch.tile([P, T * PACK], BF16, align_bytes=64)
+            x_grouped_words = x_grouped[:].bitcast(F32).rearrange("p (s u) -> p s u", u=2)
+            for pair in range(TILES // 2):
+                xT_ps = ps_misc.tile([P, 2, HALF], F32, tag="misc")
+                for j in range(2):
+                    t = 2 * pair + j
+                    for u in range(2):
+                        first = t * (D // 2) + u * P
+                        nc.tensor.transpose(
+                            xT_ps[:, u, j * P : (j + 1) * P], xc_words[:, first : first + P], ident_f32[:]
+                        )
+                nc.scalar.copy(
+                    out=x_grouped_words[:, pair * HALF : (pair + 1) * HALF, :],
+                    in_=xT_ps[:].rearrange("p u s -> p s u"),
+                )
+            x_codes = batch.tile([P, T], U32, align_bytes=64)
+            x_scales = batch.tile([P, T], U8, align_bytes=64)
+            nc.vector.quantize_mx(out=x_codes[:].bitcast(FP8X4), scales=x_scales[:], in_=x_grouped[:])
+
+            v_grouped = batch.tile([P, D, PACK], BF16, align_bytes=64)
+            for h in range(H):
+                cols = slice(h * HD, (h + 1) * HD)
+                v_ps = ps_misc.tile([P, TILES, HD], F32, tag="misc")
+                for t in range(TILES):
+                    stream = 0 if t == 0 else 1
+                    toks = slice(t * P, (t + 1) * P)
+                    nc.tensor.matmul_mx(
+                        out=v_ps[:, t, :],
+                        lhsT=x_codes[:, toks].bitcast(FP8X4),
+                        lhsT_scale=x_scales[:, toks],
+                        rhs=w_codes[:, stream, cols].bitcast(FP8X4),
+                        rhs_scale=w_scales[:, stream, cols],
+                        start=True,
+                        stop=True,
+                    )
+                nc.vector.tensor_tensor(
+                    out=v_grouped[:, cols, :],
+                    in0=v_ps[:].rearrange("p t d -> p d t"),
+                    in1=bias_grouped[:, cols, :],
+                    op=ALU.add,
+                )
+            v_codes = batch.tile([P, D], U32, align_bytes=64)
+            v_scales = batch.tile([P, D], U8, align_bytes=64)
+            nc.vector.quantize_mx(
+                out=v_codes[:].bitcast(FP8X4), scales=v_scales[:], in_=v_grouped[:].rearrange("p n t -> p (n t)")
+            )
+
+            y_sb = batch.tile([P, TILES, D], F32)
+            for h in range(H):
+                cols = slice(h * HD, (h + 1) * HD)
+                qkT_ps = ps_misc.tile([P, 2 * T], BF16, tag="misc")
+                for t in range(TILES):
+                    nc.tensor.transpose(qkT_ps[:, t * P : (t + 1) * P], q_sb[:, h * TILES + t, :], ident_bf16[:])
+                for t in range(TILES):
+                    nc.tensor.transpose(
+                        qkT_ps[:, T + t * P : T + (t + 1) * P], k_sb[:, h * TILES + t, :], ident_bf16[:]
+                    )
+                qkT = head.tile([P, 2 * T], BF16)
+                nc.scalar.copy(out=qkT[:], in_=qkT_ps[:])
+
+                rowsum = head.tile([P, TILES], F32)
+                e_grouped = head.tile([P, T * PACK], BF16, align_bytes=64)
+                e_grouped_words = e_grouped[:].bitcast(F32).rearrange("p (q u) -> p q u", u=2)
+                for pair in range(TILES // 2):
+                    eT_ps = ps_eT.tile([P, 2, HALF], F32)
+                    for j in range(2):
+                        i = 2 * pair + j
+                        s_ps = ps_scores.tile([P, T], F32)
+                        nc.tensor.matmul(
+                            out=s_ps[:], lhsT=qkT[:, i * P : (i + 1) * P], rhs=qkT[:, T:], start=True, stop=True
+                        )
+                        row_max = rows.tile([P, 1], F32)
+                        nc.vector.reduce_max(out=row_max[:], in_=s_ps[:], axis=mybir.AxisListType.X)
+                        shift = rows.tile([P, 1], F32)
+                        nc.gpsimd.tensor_scalar(
+                            out=shift[:], in0=row_max[:], scalar1=-SCALE, scalar2=0.0, op0=ALU.mult, op1=ALU.add
+                        )
+                        e_sb = rows.tile([P, T], BF16)
+                        nc.scalar.activation(
+                            out=e_sb[:].rearrange("q (u p e) -> q u p e", u=2, e=2),
+                            in_=s_ps[:].rearrange("q (u e p) -> q u p e", u=2, e=2),
+                            func=ACT.Exp,
+                            bias=shift[:],
+                            scale=SCALE,
+                            accum_out=rowsum[:, i : i + 1],
+                        )
+                        e_words = e_sb[:].bitcast(F32)
+                        for u in range(2):
+                            nc.tensor.transpose(
+                                eT_ps[:, u, j * P : (j + 1) * P], e_words[:, u * P : (u + 1) * P], ident_f32[:]
+                            )
+                    nc.scalar.copy(
+                        out=e_grouped_words[:, pair * HALF : (pair + 1) * HALF, :],
+                        in_=eT_ps[:].rearrange("p u q -> p q u"),
+                    )
+                e_codes = head.tile([P, T], U32, align_bytes=64)
+                e_scales = head.tile([P, T], U8, align_bytes=64)
+                nc.vector.quantize_mx(out=e_codes[:].bitcast(FP8X4), scales=e_scales[:], in_=e_grouped[:])
+
+                y_ps = ps_y.tile([P, TILES, HD], F32)
+                for i in range(TILES):
+                    qs = slice(i * P, (i + 1) * P)
+                    nc.tensor.matmul_mx(
+                        out=y_ps[:, i, :],
+                        lhsT=e_codes[:, qs].bitcast(FP8X4),
+                        lhsT_scale=e_scales[:, qs],
+                        rhs=v_codes[:, cols].bitcast(FP8X4),
+                        rhs_scale=v_scales[:, cols],
+                        start=True,
+                        stop=True,
+                    )
+                inv_sum = head.tile([P, TILES], F32)
+                nc.vector.reciprocal(out=inv_sum[:], in_=rowsum[:])
+                nc.vector.tensor_tensor(
+                    out=y_sb[:, :, cols],
+                    in0=y_ps[:],
+                    in1=inv_sum[:].unsqueeze(2).to_broadcast([P, TILES, HD]),
+                    op=ALU.mult,
+                )
+
+            nc.sync.dma_start(out=out_1[b], in_=y_sb[:, 0, :])
+            nc.sync.dma_start(out=out_0[b].rearrange("(t p) n -> p t n", p=P), in_=y_sb[:, 1:, :])

@@ -22,6 +22,8 @@ PACK = 4
 TILES = T // P
 HALF = 2 * P
 SCALE = 1.0 / math.sqrt(HD)
+HEADS = B * H
+ROW_TILES = HEADS * TILES
 
 FLOPS = 2 * B * T * D * D + 2 * 2 * B * H * T * T * HD
 
@@ -34,174 +36,313 @@ def tile_dualstreamattentionwithrotaryembedding_pb_t_kernel(
         const = ctx.enter_context(tc.tile_pool(name="const", bufs=1))
         loads = ctx.enter_context(tc.tile_pool(name="loads", bufs=3))
         batch = ctx.enter_context(tc.tile_pool(name="batch", bufs=2))
-        head = ctx.enter_context(tc.tile_pool(name="head", bufs=3))
+        head = ctx.enter_context(tc.tile_pool(name="head", bufs=4))
         rows = ctx.enter_context(tc.tile_pool(name="rows", bufs=6))
+        ahead = ctx.enter_context(tc.tile_pool(name="ahead", bufs=6))
         ps_scores = ctx.enter_context(tc.psum_pool(name="ps_scores", bufs=3))
         ps_eT = ctx.enter_context(tc.psum_pool(name="ps_eT", bufs=2))
         ps_y = ctx.enter_context(tc.psum_pool(name="ps_y", bufs=1))
         ps_misc = ctx.enter_context(tc.psum_pool(name="ps_misc", bufs=2))
+        ctx.enter_context(tc.manual_schedule())
+
+        live = {}
 
         ident_bf16 = const.tile([P, P], BF16)
         make_identity(nc, ident_bf16[:])
         ident_f32 = const.tile([P, P], F32)
         make_identity(nc, ident_f32[:])
 
-        w_codes = const.tile([P, 2, D], U32, align_bytes=64)
-        w_scales = const.tile([P, 2, D], U8, align_bytes=64)
-        for stream, w in enumerate((Wv_c, Wv_x)):
-            w_rows = const.tile([P, PACK * D], BF16, name="w_rows%d" % stream)
-            nc.sync.dma_start(
-                out=w_rows[:].rearrange("p (u m) -> p u m", u=2),
-                in_=w.rearrange("(u p e) n -> p u (e n)", u=2, e=2),
-            )
-            w_grouped = const.tile([P, D * PACK], BF16, name="w_grouped%d" % stream, align_bytes=64)
-            nc.vector.tensor_copy(
-                out=w_grouped[:].rearrange("p (n t) -> p n t", t=PACK),
-                in_=w_rows[:].rearrange("p (t n) -> p n t", t=PACK),
-            )
-            nc.vector.quantize_mx(
-                out=w_codes[:, stream, :].bitcast(FP8X4), scales=w_scales[:, stream, :], in_=w_grouped[:]
-            )
-
-        bias_rows = const.tile([P, 2, D], BF16)
-        nc.sync.dma_start(out=bias_rows[:, 0, :], in_=bv_c.partition_broadcast(P))
-        nc.sync.dma_start(out=bias_rows[:, 1, :], in_=bv_x.partition_broadcast(P))
-        bias_grouped = const.tile([P, D, PACK], F32)
-        nc.scalar.copy(out=bias_grouped[:], in_=bias_rows[:, 1, :].unsqueeze(2).to_broadcast([P, D, PACK]))
-        nc.scalar.copy(out=bias_grouped[:, :, 0], in_=bias_rows[:, 0, :])
-
-        for b in range(B):
+        def load_x(b):
+            if not 0 <= b < B:
+                return
             xc_sb = loads.tile([P, TILES * D], BF16)
             nc.sync.dma_start(out=xc_sb[:, 0:D], in_=c[b])
             nc.sync.dma_start(
                 out=xc_sb[:, D:].rearrange("p (t k) -> p t k", k=D),
                 in_=x[b].rearrange("(t p) k -> p t k", p=P),
             )
+            live["xc", b] = xc_sb
+
+        def load_qk(b):
+            if not 0 <= b < B:
+                return
             q_sb = loads.tile([P, H * TILES, HD], BF16)
             nc.sync.dma_start(out=q_sb[:], in_=q_rot[b].rearrange("h (t p) d -> p (h t) d", p=P))
             k_sb = loads.tile([P, H * TILES, HD], BF16)
             nc.sync.dma_start(out=k_sb[:], in_=k_rot[b].rearrange("h (t p) d -> p (h t) d", p=P))
+            live["q", b] = q_sb
+            live["k", b] = k_sb
 
-            xc_words = xc_sb[:].bitcast(F32)
-            x_grouped = batch.tile([P, T * PACK], BF16, align_bytes=64)
-            x_grouped_words = x_grouped[:].bitcast(F32).rearrange("p (s u) -> p s u", u=2)
-            for pair in range(TILES // 2):
-                xT_ps = ps_misc.tile([P, 2, HALF], F32, tag="misc")
-                for j in range(2):
-                    t = 2 * pair + j
-                    for u in range(2):
-                        first = t * (D // 2) + u * P
-                        nc.tensor.transpose(
-                            xT_ps[:, u, j * P : (j + 1) * P], xc_words[:, first : first + P], ident_f32[:]
-                        )
-                nc.scalar.copy(
-                    out=x_grouped_words[:, pair * HALF : (pair + 1) * HALF, :],
-                    in_=xT_ps[:].rearrange("p u s -> p s u"),
-                )
-            x_codes = batch.tile([P, T], U32, align_bytes=64)
-            x_scales = batch.tile([P, T], U8, align_bytes=64)
-            nc.vector.quantize_mx(out=x_codes[:].bitcast(FP8X4), scales=x_scales[:], in_=x_grouped[:])
-
-            v_grouped = batch.tile([P, D, PACK], BF16, align_bytes=64)
-            for h in range(H):
-                cols = slice(h * HD, (h + 1) * HD)
-                v_ps = ps_misc.tile([P, TILES, HD], F32, tag="misc")
-                for t in range(TILES):
-                    stream = 0 if t == 0 else 1
-                    toks = slice(t * P, (t + 1) * P)
-                    nc.tensor.matmul_mx(
-                        out=v_ps[:, t, :],
-                        lhsT=x_codes[:, toks].bitcast(FP8X4),
-                        lhsT_scale=x_scales[:, toks],
-                        rhs=w_codes[:, stream, cols].bitcast(FP8X4),
-                        rhs_scale=w_scales[:, stream, cols],
-                        start=True,
-                        stop=True,
-                    )
-                nc.vector.tensor_tensor(
-                    out=v_grouped[:, cols, :],
-                    in0=v_ps[:].rearrange("p t d -> p d t"),
-                    in1=bias_grouped[:, cols, :],
-                    op=ALU.add,
-                )
-            v_codes = batch.tile([P, D], U32, align_bytes=64)
-            v_scales = batch.tile([P, D], U8, align_bytes=64)
-            nc.vector.quantize_mx(
-                out=v_codes[:].bitcast(FP8X4), scales=v_scales[:], in_=v_grouped[:].rearrange("p n t -> p (n t)")
-            )
-
-            y_sb = batch.tile([P, TILES, D], F32)
-            for h in range(H):
-                cols = slice(h * HD, (h + 1) * HD)
-                qkT_ps = ps_misc.tile([P, 2 * T], BF16, tag="misc")
-                for t in range(TILES):
-                    nc.tensor.transpose(qkT_ps[:, t * P : (t + 1) * P], q_sb[:, h * TILES + t, :], ident_bf16[:])
-                for t in range(TILES):
-                    nc.tensor.transpose(
-                        qkT_ps[:, T + t * P : T + (t + 1) * P], k_sb[:, h * TILES + t, :], ident_bf16[:]
-                    )
-                qkT = head.tile([P, 2 * T], BF16)
-                nc.scalar.copy(out=qkT[:], in_=qkT_ps[:])
-
-                rowsum = head.tile([P, TILES], F32)
-                e_grouped = head.tile([P, T * PACK], BF16, align_bytes=64)
-                e_grouped_words = e_grouped[:].bitcast(F32).rearrange("p (q u) -> p q u", u=2)
-                for pair in range(TILES // 2):
-                    eT_ps = ps_eT.tile([P, 2, HALF], F32)
-                    for j in range(2):
-                        i = 2 * pair + j
-                        s_ps = ps_scores.tile([P, T], F32)
-                        nc.tensor.matmul(
-                            out=s_ps[:], lhsT=qkT[:, i * P : (i + 1) * P], rhs=qkT[:, T:], start=True, stop=True
-                        )
-                        row_max = rows.tile([P, 1], F32)
-                        nc.vector.reduce_max(out=row_max[:], in_=s_ps[:], axis=mybir.AxisListType.X)
-                        shift = rows.tile([P, 1], F32)
-                        nc.gpsimd.tensor_scalar(
-                            out=shift[:], in0=row_max[:], scalar1=-SCALE, scalar2=0.0, op0=ALU.mult, op1=ALU.add
-                        )
-                        e_sb = rows.tile([P, T], BF16)
-                        nc.scalar.activation(
-                            out=e_sb[:].rearrange("q (u p e) -> q u p e", u=2, e=2),
-                            in_=s_ps[:].rearrange("q (u e p) -> q u p e", u=2, e=2),
-                            func=ACT.Exp,
-                            bias=shift[:],
-                            scale=SCALE,
-                            accum_out=rowsum[:, i : i + 1],
-                        )
-                        e_words = e_sb[:].bitcast(F32)
-                        for u in range(2):
-                            nc.tensor.transpose(
-                                eT_ps[:, u, j * P : (j + 1) * P], e_words[:, u * P : (u + 1) * P], ident_f32[:]
-                            )
-                    nc.scalar.copy(
-                        out=e_grouped_words[:, pair * HALF : (pair + 1) * HALF, :],
-                        in_=eT_ps[:].rearrange("p u q -> p q u"),
-                    )
-                e_codes = head.tile([P, T], U32, align_bytes=64)
-                e_scales = head.tile([P, T], U8, align_bytes=64)
-                nc.vector.quantize_mx(out=e_codes[:].bitcast(FP8X4), scales=e_scales[:], in_=e_grouped[:])
-
-                y_ps = ps_y.tile([P, TILES, HD], F32)
-                for i in range(TILES):
-                    qs = slice(i * P, (i + 1) * P)
-                    nc.tensor.matmul_mx(
-                        out=y_ps[:, i, :],
-                        lhsT=e_codes[:, qs].bitcast(FP8X4),
-                        lhsT_scale=e_scales[:, qs],
-                        rhs=v_codes[:, cols].bitcast(FP8X4),
-                        rhs_scale=v_scales[:, cols],
-                        start=True,
-                        stop=True,
-                    )
-                inv_sum = head.tile([P, TILES], F32)
-                nc.vector.reciprocal(out=inv_sum[:], in_=rowsum[:])
-                nc.vector.tensor_tensor(
-                    out=y_sb[:, :, cols],
-                    in0=y_ps[:],
-                    in1=inv_sum[:].unsqueeze(2).to_broadcast([P, TILES, HD]),
-                    op=ALU.mult,
-                )
-
+        def store_y(b):
+            if not 0 <= b < B:
+                return
+            y_sb = live["y", b]
             nc.sync.dma_start(out=out_1[b], in_=y_sb[:, 0, :])
             nc.sync.dma_start(out=out_0[b].rearrange("(t p) n -> p t n", p=P), in_=y_sb[:, 1:, :])
+
+        w_codes = const.tile([P, 2, D], U32, align_bytes=64)
+        w_scales = const.tile([P, 2, D], U8, align_bytes=64)
+        w_rows = const.tile([P, 2, PACK * D], BF16)
+        for stream, w in enumerate((Wv_c, Wv_x)):
+            nc.sync.dma_start(
+                out=w_rows[:, stream, :].rearrange("p (u m) -> p u m", u=2),
+                in_=w.rearrange("(u p e) n -> p u (e n)", u=2, e=2),
+            )
+        load_x(0)
+        bias_rows = const.tile([P, 2, D], BF16)
+        nc.sync.dma_start(out=bias_rows[:, 0, :], in_=bv_c.partition_broadcast(P))
+        nc.sync.dma_start(out=bias_rows[:, 1, :], in_=bv_x.partition_broadcast(P))
+        w_grouped = const.tile([P, 2, D * PACK], BF16, align_bytes=64)
+        for stream in range(2):
+            nc.vector.tensor_copy(
+                out=w_grouped[:, stream, :].rearrange("p (n t) -> p n t", t=PACK),
+                in_=w_rows[:, stream, :].rearrange("p (t n) -> p n t", t=PACK),
+            )
+        for stream in range(2):
+            nc.vector.quantize_mx(
+                out=w_codes[:, stream, :].bitcast(FP8X4), scales=w_scales[:, stream, :], in_=w_grouped[:, stream, :]
+            )
+        bias_grouped = const.tile([P, D, PACK], F32)
+        nc.scalar.copy(out=bias_grouped[:], in_=bias_rows[:, 1, :].unsqueeze(2).to_broadcast([P, D, PACK]))
+        nc.scalar.copy(out=bias_grouped[:, :, 0], in_=bias_rows[:, 0, :])
+
+        def transpose_x(xt):
+            if not 0 <= xt < B * TILES:
+                return
+            b, t = divmod(xt, TILES)
+            xc_words = live["xc", b][:].bitcast(F32)
+            xT_ps = ps_misc.tile([P, 2, P], F32, tag="misc")
+            for u in range(2):
+                first = t * (D // 2) + u * P
+                nc.tensor.transpose(xT_ps[:, u, :], xc_words[:, first : first + P], ident_f32[:])
+            live["xT_ps", xt] = xT_ps
+
+        def copy_xT(xt):
+            if not 0 <= xt < B * TILES:
+                return
+            x_grouped = head.tile([P, P * PACK], BF16, align_bytes=64)
+            nc.scalar.copy(
+                out=x_grouped[:].bitcast(F32).rearrange("p (s u) -> p s u", u=2),
+                in_=live["xT_ps", xt][:].rearrange("p u s -> p s u"),
+            )
+            live["x_grouped", xt] = x_grouped
+
+        def quantise_x(xt):
+            if not 0 <= xt < B * TILES:
+                return
+            b, t = divmod(xt, TILES)
+            if t == 0:
+                x_codes = batch.tile([P, T], U32, align_bytes=64)
+                x_scales = batch.tile([P, T], U8, align_bytes=64)
+                live["x_codes", b] = x_codes
+                live["x_scales", b] = x_scales
+            toks = slice(t * P, (t + 1) * P)
+            nc.vector.quantize_mx(
+                out=live["x_codes", b][:, toks].bitcast(FP8X4),
+                scales=live["x_scales", b][:, toks],
+                in_=live["x_grouped", xt][:],
+            )
+
+        def project_v(n):
+            if not 0 <= n < HEADS:
+                return
+            b, h = divmod(n, H)
+            cols = slice(h * HD, (h + 1) * HD)
+            v_ps = ps_misc.tile([P, TILES, HD], F32, tag="misc")
+            for t in range(TILES):
+                stream = 0 if t == 0 else 1
+                toks = slice(t * P, (t + 1) * P)
+                nc.tensor.matmul_mx(
+                    out=v_ps[:, t, :],
+                    lhsT=live["x_codes", b][:, toks].bitcast(FP8X4),
+                    lhsT_scale=live["x_scales", b][:, toks],
+                    rhs=w_codes[:, stream, cols].bitcast(FP8X4),
+                    rhs_scale=w_scales[:, stream, cols],
+                    start=True,
+                    stop=True,
+                )
+            live["v_ps", n] = v_ps
+
+        def add_bias_v(n):
+            if not 0 <= n < HEADS:
+                return
+            h = n % H
+            v_grouped = head.tile([P, HD, PACK], BF16, align_bytes=64)
+            nc.vector.tensor_tensor(
+                out=v_grouped[:],
+                in0=live["v_ps", n][:].rearrange("p t d -> p d t"),
+                in1=bias_grouped[:, h * HD : (h + 1) * HD, :],
+                op=ALU.add,
+            )
+            live["v_grouped", n] = v_grouped
+
+        def quantise_v(n):
+            if not 0 <= n < HEADS:
+                return
+            v_codes = ahead.tile([P, HD], U32, align_bytes=64)
+            v_scales = ahead.tile([P, HD], U8, align_bytes=64)
+            nc.vector.quantize_mx(
+                out=v_codes[:].bitcast(FP8X4),
+                scales=v_scales[:],
+                in_=live["v_grouped", n][:].rearrange("p d t -> p (d t)"),
+            )
+            live["v_codes", n] = v_codes
+            live["v_scales", n] = v_scales
+
+        def transpose_qk(n):
+            if not 0 <= n < HEADS:
+                return
+            b, h = divmod(n, H)
+            qkT_ps = ps_misc.tile([P, 2 * T], BF16, tag="misc")
+            for t in range(TILES):
+                nc.tensor.transpose(qkT_ps[:, t * P : (t + 1) * P], live["q", b][:, h * TILES + t, :], ident_bf16[:])
+            for t in range(TILES):
+                nc.tensor.transpose(
+                    qkT_ps[:, T + t * P : T + (t + 1) * P], live["k", b][:, h * TILES + t, :], ident_bf16[:]
+                )
+            live["qkT_ps", n] = qkT_ps
+
+        def copy_qkT(n):
+            if not 0 <= n < HEADS:
+                return
+            qkT = head.tile([P, 2 * T], BF16)
+            nc.scalar.copy(out=qkT[:], in_=live["qkT_ps", n][:])
+            live["qkT", n] = qkT
+
+        def scores(k):
+            if not 0 <= k < ROW_TILES:
+                return
+            n, i = divmod(k, TILES)
+            qkT = live["qkT", n]
+            s_ps = ps_scores.tile([P, T], F32)
+            nc.tensor.matmul(out=s_ps[:], lhsT=qkT[:, i * P : (i + 1) * P], rhs=qkT[:, T:], start=True, stop=True)
+            live["s_ps", k] = s_ps
+
+        def row_maximum(k):
+            if not 0 <= k < ROW_TILES:
+                return
+            row_max = rows.tile([P, 1], F32)
+            nc.vector.reduce_max(out=row_max[:], in_=live["s_ps", k][:], axis=mybir.AxisListType.X)
+            shift = rows.tile([P, 1], F32)
+            nc.gpsimd.tensor_scalar(
+                out=shift[:], in0=row_max[:], scalar1=-SCALE, scalar2=0.0, op0=ALU.mult, op1=ALU.add
+            )
+            live["shift", k] = shift
+
+        def exponentials(k):
+            if not 0 <= k < ROW_TILES:
+                return
+            n, i = divmod(k, TILES)
+            if i == 0:
+                rowsum = head.tile([P, TILES], F32)
+                live["rowsum", n] = rowsum
+            e_sb = rows.tile([P, T], BF16)
+            nc.scalar.activation(
+                out=e_sb[:].rearrange("q (u p e) -> q u p e", u=2, e=2),
+                in_=live["s_ps", k][:].rearrange("q (u e p) -> q u p e", u=2, e=2),
+                func=ACT.Exp,
+                bias=live["shift", k][:],
+                scale=SCALE,
+                accum_out=live["rowsum", n][:, i : i + 1],
+            )
+            live["e", k] = e_sb
+
+        def transpose_e(n, pair):
+            if not 0 <= n < HEADS:
+                return
+            eT_ps = ps_eT.tile([P, 2, HALF], F32)
+            for j in range(2):
+                e_words = live["e", n * TILES + 2 * pair + j][:].bitcast(F32)
+                for u in range(2):
+                    nc.tensor.transpose(eT_ps[:, u, j * P : (j + 1) * P], e_words[:, u * P : (u + 1) * P], ident_f32[:])
+            live["eT_ps", n, pair] = eT_ps
+
+        def copy_eT(n, pair):
+            if not 0 <= n < HEADS:
+                return
+            if pair == 0:
+                e_grouped = head.tile([P, T * PACK], BF16, align_bytes=64)
+                live["e_grouped", n] = e_grouped
+            e_grouped_words = live["e_grouped", n][:].bitcast(F32).rearrange("p (q u) -> p q u", u=2)
+            nc.scalar.copy(
+                out=e_grouped_words[:, pair * HALF : (pair + 1) * HALF, :],
+                in_=live["eT_ps", n, pair][:].rearrange("p u q -> p q u"),
+            )
+
+        def quantise_e(n):
+            if not 0 <= n < HEADS:
+                return
+            e_codes = head.tile([P, T], U32, align_bytes=64)
+            e_scales = head.tile([P, T], U8, align_bytes=64)
+            nc.vector.quantize_mx(out=e_codes[:].bitcast(FP8X4), scales=e_scales[:], in_=live["e_grouped", n][:])
+            live["e_codes", n] = e_codes
+            live["e_scales", n] = e_scales
+
+        def multiply_ev(n):
+            if not 0 <= n < HEADS:
+                return
+            y_ps = ps_y.tile([P, TILES, HD], F32)
+            for i in range(TILES):
+                qs = slice(i * P, (i + 1) * P)
+                nc.tensor.matmul_mx(
+                    out=y_ps[:, i, :],
+                    lhsT=live["e_codes", n][:, qs].bitcast(FP8X4),
+                    lhsT_scale=live["e_scales", n][:, qs],
+                    rhs=live["v_codes", n][:].bitcast(FP8X4),
+                    rhs_scale=live["v_scales", n][:],
+                    start=True,
+                    stop=True,
+                )
+            live["y_ps", n] = y_ps
+
+        def normalise(n):
+            if not 0 <= n < HEADS:
+                return
+            b, h = divmod(n, H)
+            if h == 0:
+                y_sb = batch.tile([P, TILES, D], F32)
+                live["y", b] = y_sb
+            inv_sum = head.tile([P, TILES], F32)
+            nc.vector.reciprocal(out=inv_sum[:], in_=live["rowsum", n][:])
+            nc.vector.tensor_tensor(
+                out=live["y", b][:, :, h * HD : (h + 1) * HD],
+                in0=live["y_ps", n][:],
+                in1=inv_sum[:].unsqueeze(2).to_broadcast([P, TILES, HD]),
+                op=ALU.mult,
+            )
+            if h == H - 1:
+                store_y(b)
+
+        for n in range(-2 * H, HEADS + 2):
+            b, h = divmod(n, H)
+            k = n * TILES
+            if h == 0:
+                load_qk(b + 2)
+                load_x(b + 3)
+            transpose_e(n - 1, 1)
+            scores(k + 2)
+            row_maximum(k + 1)
+            normalise(n - 2)
+            exponentials(k)
+            copy_xT(n + 7)
+            scores(k + 3)
+            transpose_qk(n + 2)
+            row_maximum(k + 2)
+            quantise_x(n + 7)
+            quantise_v(n + 3)
+            exponentials(k + 1)
+            copy_eT(n - 1, 1)
+            transpose_e(n, 0)
+            scores(k + 4)
+            project_v(n + 4)
+            row_maximum(k + 3)
+            quantise_e(n - 1)
+            exponentials(k + 2)
+            copy_qkT(n + 2)
+            multiply_ev(n - 1)
+            scores(k + 5)
+            transpose_x(n + 8)
+            row_maximum(k + 4)
+            add_bias_v(n + 4)
+            exponentials(k + 3)
+            copy_eT(n, 0)

@@ -295,6 +295,13 @@ def tile_dualstreamattentionwithrotaryembedding_pb_t_kernel(
                 )
             live["y_ps", n] = y_ps
 
+        def invert_sums(n):
+            if not 0 <= n < HEADS:
+                return
+            inv_sum = head.tile([P, TILES], F32)
+            nc.vector.reciprocal(out=inv_sum[:], in_=live["rowsum", n][:])
+            live["inv_sum", n] = inv_sum
+
         def normalise(n):
             if not 0 <= n < HEADS:
                 return
@@ -302,12 +309,10 @@ def tile_dualstreamattentionwithrotaryembedding_pb_t_kernel(
             if h == 0:
                 y_sb = batch.tile([P, TILES, D], F32)
                 live["y", b] = y_sb
-            inv_sum = head.tile([P, TILES], F32)
-            nc.vector.reciprocal(out=inv_sum[:], in_=live["rowsum", n][:])
             nc.vector.tensor_tensor(
                 out=live["y", b][:, :, h * HD : (h + 1) * HD],
                 in0=live["y_ps", n][:],
-                in1=inv_sum[:].unsqueeze(2).to_broadcast([P, TILES, HD]),
+                in1=live["inv_sum", n][:].unsqueeze(2).to_broadcast([P, TILES, HD]),
                 op=ALU.mult,
             )
             if h == H - 1:
@@ -344,5 +349,6 @@ def tile_dualstreamattentionwithrotaryembedding_pb_t_kernel(
             transpose_x(n + 8)
             row_maximum(k + 4)
             add_bias_v(n + 4)
+            invert_sums(n - 1)
             exponentials(k + 3)
             copy_eT(n, 0)

@@ -25,6 +25,7 @@ SCALE = 1.0 / math.sqrt(HD)
 HEADS = B * H
 ROW_TILES = HEADS * TILES
 
+V_FIRST = 1
 FLOPS = 2 * B * T * D * D + 2 * 2 * B * H * T * T * HD
 
 
@@ -39,14 +40,20 @@ def tile_dualstreamattentionwithrotaryembedding_pb_t_kernel(
         head = ctx.enter_context(tc.tile_pool(name="head", bufs=4))
         rows = ctx.enter_context(tc.tile_pool(name="rows", bufs=6))
         ahead = ctx.enter_context(tc.tile_pool(name="ahead", bufs=6))
-        ps_scores = ctx.enter_context(tc.psum_pool(name="ps_scores", bufs=3))
-        ps_eT = ctx.enter_context(tc.psum_pool(name="ps_eT", bufs=2))
+        ps_scores = ctx.enter_context(tc.psum_pool(name="ps_scores", bufs=4))
+        ps_eT = ctx.enter_context(tc.psum_pool(name="ps_eT", bufs=1))
         ps_y = ctx.enter_context(tc.psum_pool(name="ps_y", bufs=1))
         ps_misc = ctx.enter_context(tc.psum_pool(name="ps_misc", bufs=2))
         ctx.enter_context(tc.manual_schedule())
 
         live = {}
 
+        warm = const.tile([P, 1], F32)
+        nc.gpsimd.memset(warm[:], 0.0)
+        warm_exp = const.tile([P, 1], F32)
+        nc.scalar.activation(out=warm_exp[:], in_=warm[:], func=ACT.Exp)
+        minus_one = const.tile([P, TILES], F32)
+        nc.gpsimd.memset(minus_one[:], -1.0)
         ident_bf16 = const.tile([P, P], BF16)
         make_identity(nc, ident_bf16[:])
         ident_f32 = const.tile([P, P], F32)
@@ -67,11 +74,17 @@ def tile_dualstreamattentionwithrotaryembedding_pb_t_kernel(
             if not 0 <= b < B:
                 return
             q_sb = loads.tile([P, H * TILES, HD], BF16)
-            nc.sync.dma_start(out=q_sb[:], in_=q_rot[b].rearrange("h (t p) d -> p (h t) d", p=P))
             k_sb = loads.tile([P, H * TILES, HD], BF16)
-            nc.sync.dma_start(out=k_sb[:], in_=k_rot[b].rearrange("h (t p) d -> p (h t) d", p=P))
             live["q", b] = q_sb
             live["k", b] = k_sb
+            load_qk_heads(b, 0, 1 if b == 0 else H)
+
+        def load_qk_heads(b, first, last):
+            for name, src in (("q", q_rot), ("k", k_rot)):
+                nc.sync.dma_start(
+                    out=live[name, b][:, first * TILES : last * TILES, :],
+                    in_=src[b, first:last].rearrange("h (t p) d -> p (h t) d", p=P),
+                )
 
         def store_y(b):
             if not 0 <= b < B:
@@ -80,6 +93,7 @@ def tile_dualstreamattentionwithrotaryembedding_pb_t_kernel(
             nc.sync.dma_start(out=out_1[b], in_=y_sb[:, 0, :])
             nc.sync.dma_start(out=out_0[b].rearrange("(t p) n -> p t n", p=P), in_=y_sb[:, 1:, :])
 
+        load_qk(0)
         w_codes = const.tile([P, 2, D], U32, align_bytes=64)
         w_scales = const.tile([P, 2, D], U8, align_bytes=64)
         w_rows = const.tile([P, 2, PACK * D], BF16)
@@ -88,59 +102,89 @@ def tile_dualstreamattentionwithrotaryembedding_pb_t_kernel(
                 out=w_rows[:, stream, :].rearrange("p (u m) -> p u m", u=2),
                 in_=w.rearrange("(u p e) n -> p u (e n)", u=2, e=2),
             )
+        load_qk_heads(0, 1, 2)
         load_x(0)
+        load_qk_heads(0, 2, H)
         bias_rows = const.tile([P, 2, D], BF16)
         nc.sync.dma_start(out=bias_rows[:, 0, :], in_=bv_c.partition_broadcast(P))
         nc.sync.dma_start(out=bias_rows[:, 1, :], in_=bv_x.partition_broadcast(P))
         w_grouped = const.tile([P, 2, D * PACK], BF16, align_bytes=64)
-        for stream in range(2):
+
+        def group_w_c():
             nc.vector.tensor_copy(
-                out=w_grouped[:, stream, :].rearrange("p (n t) -> p n t", t=PACK),
-                in_=w_rows[:, stream, :].rearrange("p (t n) -> p n t", t=PACK),
+                out=w_grouped[:, 0, :].rearrange("p (n t) -> p n t", t=PACK),
+                in_=w_rows[:, 0, :].rearrange("p (t n) -> p n t", t=PACK),
             )
-        for stream in range(2):
+
+        def group_w_x(h):
+            cols = slice(h * HD, (h + 1) * HD)
+            nc.gpsimd.tensor_scalar(
+                out=w_grouped[:, 1, :].rearrange("p (n t) -> p n t", t=PACK)[:, cols, :],
+                in0=w_rows[:, 1, :].rearrange("p (t n) -> p n t", t=PACK)[:, cols, :],
+                scalar1=1.0, scalar2=0.0, op0=ALU.mult, op1=ALU.add,
+            )
+
+        def quantise_w(stream):
             nc.vector.quantize_mx(
                 out=w_codes[:, stream, :].bitcast(FP8X4), scales=w_scales[:, stream, :], in_=w_grouped[:, stream, :]
             )
+
         bias_grouped = const.tile([P, D, PACK], F32)
-        nc.scalar.copy(out=bias_grouped[:], in_=bias_rows[:, 1, :].unsqueeze(2).to_broadcast([P, D, PACK]))
-        nc.scalar.copy(out=bias_grouped[:, :, 0], in_=bias_rows[:, 0, :])
 
-        def transpose_x(xt):
-            if not 0 <= xt < B * TILES:
+        def group_bias(h):
+            cols = slice(h * HD, (h + 1) * HD)
+            nc.gpsimd.tensor_scalar(
+                out=bias_grouped[:, cols, :],
+                in0=bias_rows[:, 1, cols].unsqueeze(2).to_broadcast([P, HD, PACK]),
+                scalar1=1.0, scalar2=0.0, op0=ALU.mult, op1=ALU.add,
+            )
+            nc.gpsimd.tensor_scalar(
+                out=bias_grouped[:, cols, 0],
+                in0=bias_rows[:, 0, cols],
+                scalar1=1.0, scalar2=0.0, op0=ALU.mult, op1=ALU.add,
+            )
+
+        load_qk(1)
+        load_x(1)
+
+        def transpose_x(xp):
+            if not 0 <= xp < 2 * B:
                 return
-            b, t = divmod(xt, TILES)
+            b, pair = divmod(xp, 2)
             xc_words = live["xc", b][:].bitcast(F32)
-            xT_ps = ps_misc.tile([P, 2, P], F32, tag="misc")
-            for u in range(2):
-                first = t * (D // 2) + u * P
-                nc.tensor.transpose(xT_ps[:, u, :], xc_words[:, first : first + P], ident_f32[:])
-            live["xT_ps", xt] = xT_ps
+            xT_ps = ps_misc.tile([P, 2, HALF], F32, tag="misc")
+            for j in range(2):
+                for u in range(2):
+                    first = (2 * pair + j) * (D // 2) + u * P
+                    nc.tensor.transpose(
+                        xT_ps[:, u, j * P : (j + 1) * P], xc_words[:, first : first + P], ident_f32[:]
+                    )
+            live["xT_ps", xp] = xT_ps
 
-        def copy_xT(xt):
-            if not 0 <= xt < B * TILES:
+        def copy_xT(xp):
+            if not 0 <= xp < 2 * B:
                 return
-            x_grouped = head.tile([P, P * PACK], BF16, align_bytes=64)
+            x_grouped = head.tile([P, HALF * PACK], BF16, align_bytes=64)
             nc.scalar.copy(
                 out=x_grouped[:].bitcast(F32).rearrange("p (s u) -> p s u", u=2),
-                in_=live["xT_ps", xt][:].rearrange("p u s -> p s u"),
+                in_=live["xT_ps", xp][:].rearrange("p u s -> p s u"),
             )
-            live["x_grouped", xt] = x_grouped
+            live["x_grouped", xp] = x_grouped
 
-        def quantise_x(xt):
-            if not 0 <= xt < B * TILES:
+        def quantise_x(xp):
+            if not 0 <= xp < 2 * B:
                 return
-            b, t = divmod(xt, TILES)
-            if t == 0:
+            b, pair = divmod(xp, 2)
+            if pair == 0:
                 x_codes = batch.tile([P, T], U32, align_bytes=64)
                 x_scales = batch.tile([P, T], U8, align_bytes=64)
                 live["x_codes", b] = x_codes
                 live["x_scales", b] = x_scales
-            toks = slice(t * P, (t + 1) * P)
+            toks = slice(pair * HALF, (pair + 1) * HALF)
             nc.vector.quantize_mx(
                 out=live["x_codes", b][:, toks].bitcast(FP8X4),
                 scales=live["x_scales", b][:, toks],
-                in_=live["x_grouped", xt][:],
+                in_=live["x_grouped", xp][:],
             )
 
         def project_v(n):
@@ -206,7 +250,11 @@ def tile_dualstreamattentionwithrotaryembedding_pb_t_kernel(
             if not 0 <= n < HEADS:
                 return
             qkT = head.tile([P, 2 * T], BF16)
-            nc.scalar.copy(out=qkT[:], in_=live["qkT_ps", n][:])
+            if n == 0:
+                nc.vector.tensor_copy(out=qkT[:, :T], in_=live["qkT_ps", n][:, :T])
+                nc.scalar.copy(out=qkT[:, T:], in_=live["qkT_ps", n][:, T:])
+            else:
+                nc.scalar.copy(out=qkT[:], in_=live["qkT_ps", n][:])
             live["qkT", n] = qkT
 
         def scores(k):
@@ -299,7 +347,7 @@ def tile_dualstreamattentionwithrotaryembedding_pb_t_kernel(
             if not 0 <= n < HEADS:
                 return
             inv_sum = head.tile([P, TILES], F32)
-            nc.vector.reciprocal(out=inv_sum[:], in_=live["rowsum", n][:])
+            nc.gpsimd.tensor_tensor(out=inv_sum[:], in0=live["rowsum", n][:], in1=minus_one[:], op=ALU.pow)
             live["inv_sum", n] = inv_sum
 
         def normalise(n):
@@ -309,46 +357,78 @@ def tile_dualstreamattentionwithrotaryembedding_pb_t_kernel(
             if h == 0:
                 y_sb = batch.tile([P, TILES, D], F32)
                 live["y", b] = y_sb
+            inv_sum = live["inv_sum", n]
             nc.vector.tensor_tensor(
                 out=live["y", b][:, :, h * HD : (h + 1) * HD],
                 in0=live["y_ps", n][:],
-                in1=live["inv_sum", n][:].unsqueeze(2).to_broadcast([P, TILES, HD]),
+                in1=inv_sum[:].unsqueeze(2).to_broadcast([P, TILES, HD]),
                 op=ALU.mult,
             )
             if h == H - 1:
                 store_y(b)
 
-        for n in range(-2 * H, HEADS + 2):
+        transpose_qk(0)
+        copy_qkT(0)
+        group_w_c()
+        group_w_x(0)
+        group_w_x(1)
+        for n in range(-1, HEADS + 2):
             b, h = divmod(n, H)
             k = n * TILES
             if h == 0:
                 load_qk(b + 2)
-                load_x(b + 3)
-            transpose_e(n - 1, 1)
-            scores(k + 2)
-            row_maximum(k + 1)
-            normalise(n - 2)
-            exponentials(k)
-            copy_xT(n + 7)
+                load_x(b + 2)
+            v_heads = [m for m in range(HEADS) if max(m, V_FIRST) == n]
+            first = n == 0
+            xp = (n + 3) // 2 if n > 0 and n % 2 == 1 else -1
             scores(k + 3)
-            transpose_qk(n + 2)
+            transpose_e(n - 1, 1)
+            for m in v_heads:
+                project_v(m)
             row_maximum(k + 2)
-            quantise_x(n + 7)
-            quantise_v(n + 3)
-            exponentials(k + 1)
-            copy_eT(n - 1, 1)
-            transpose_e(n, 0)
+            normalise(n - 2)
+            if first:
+                transpose_x(0)
+                quantise_w(0)
+                group_w_x(2)
+            exponentials(k)
+            if first: copy_qkT(1)
+            copy_xT(xp)
             scores(k + 4)
-            project_v(n + 4)
             row_maximum(k + 3)
-            quantise_e(n - 1)
-            exponentials(k + 2)
-            copy_qkT(n + 2)
-            multiply_ev(n - 1)
+            for m in v_heads:
+                add_bias_v(m)
+            if n>=0: transpose_qk(n + 2)
+            exponentials(k + 1)
+            if first:
+                group_w_x(3)
+                copy_xT(0)
+                transpose_x(1)
+            copy_eT(n - 1, 1)
             scores(k + 5)
-            transpose_x(n + 8)
+            transpose_e(n, 0)
             row_maximum(k + 4)
-            add_bias_v(n + 4)
+            quantise_e(n - 1)
+            if first:
+                quantise_x(0)
+                quantise_w(1)
+                group_bias(0)
+            exponentials(k + 2)
+            if n>=0: copy_qkT(n + 2)
+            if first:
+                copy_xT(1)
+            scores(k + 6)
+            if n<0: transpose_qk(n+2)
+            row_maximum(k + 5)
+            for m in v_heads:
+                quantise_v(m)
+            if first:
+                quantise_x(1)
+            quantise_x(xp)
+            if 0<=n<H-1:
+                group_bias(n+1)
+            multiply_ev(n - 1)
             invert_sums(n - 1)
+            if n>=0 and n%2==0: transpose_x((n + 4)//2)
             exponentials(k + 3)
             copy_eT(n, 0)

@@ -22,10 +22,10 @@ PACK = 4
 TILES = T // P
 HALF = 2 * P
 SCALE = 1.0 / math.sqrt(HD)
+LAST = B * H - 1
 HEADS = B * H
 ROW_TILES = HEADS * TILES
 
-V_FIRST = 1
 FLOPS = 2 * B * T * D * D + 2 * 2 * B * H * T * T * HD
 
 
@@ -52,8 +52,6 @@ def tile_dualstreamattentionwithrotaryembedding_pb_t_kernel(
         nc.gpsimd.memset(warm[:], 0.0)
         warm_exp = const.tile([P, 1], F32)
         nc.scalar.activation(out=warm_exp[:], in_=warm[:], func=ACT.Exp)
-        minus_one = const.tile([P, TILES], F32)
-        nc.gpsimd.memset(minus_one[:], -1.0)
         ident_bf16 = const.tile([P, P], BF16)
         make_identity(nc, ident_bf16[:])
         ident_f32 = const.tile([P, P], F32)
@@ -80,11 +78,18 @@ def tile_dualstreamattentionwithrotaryembedding_pb_t_kernel(
             load_qk_heads(b, 0, 1 if b == 0 else H)
 
         def load_qk_heads(b, first, last):
-            for name, src in (("q", q_rot), ("k", k_rot)):
+            for name, src in (("k", k_rot), ("q", q_rot)):
                 nc.sync.dma_start(
                     out=live[name, b][:, first * TILES : last * TILES, :],
                     in_=src[b, first:last].rearrange("h (t p) d -> p (h t) d", p=P),
                 )
+
+        def store_head(n):
+            b, h = divmod(n, H)
+            cols = slice(h * HD, (h + 1) * HD)
+            y_head = live["y_head", n]
+            nc.sync.dma_start(out=out_0[b].rearrange("(t p) n -> p t n", p=P)[:, :, cols], in_=y_head[:, 1:, :])
+            nc.sync.dma_start(out=out_1[b][:, cols], in_=y_head[:, 0, :])
 
         def store_y(b):
             if not 0 <= b < B:
@@ -238,21 +243,25 @@ def tile_dualstreamattentionwithrotaryembedding_pb_t_kernel(
                 return
             b, h = divmod(n, H)
             qkT_ps = ps_misc.tile([P, 2 * T], BF16, tag="misc")
-            for t in range(TILES):
-                nc.tensor.transpose(qkT_ps[:, t * P : (t + 1) * P], live["q", b][:, h * TILES + t, :], ident_bf16[:])
-            for t in range(TILES):
-                nc.tensor.transpose(
-                    qkT_ps[:, T + t * P : T + (t + 1) * P], live["k", b][:, h * TILES + t, :], ident_bf16[:]
-                )
             live["qkT_ps", n] = qkT_ps
+            for t in range(TILES):
+                nc.tensor.transpose(qkT_ps[:, t * P : (t + 1) * P], live["k", b][:, h * TILES + t, :], ident_bf16[:])
+            if n == 0:
+                qkT_ps = ps_misc.tile([P, 2 * T], BF16, tag="misc")
+                live["q_rest_ps"] = qkT_ps
+            for t in range(TILES):
+                bank = live["qkT_ps", n] if t == 0 else qkT_ps
+                nc.tensor.transpose(
+                    bank[:, T + t * P : T + (t + 1) * P], live["q", b][:, h * TILES + t, :], ident_bf16[:]
+                )
 
         def copy_qkT(n):
             if not 0 <= n < HEADS:
                 return
             qkT = head.tile([P, 2 * T], BF16)
             if n == 0:
-                nc.vector.tensor_copy(out=qkT[:, :T], in_=live["qkT_ps", n][:, :T])
-                nc.scalar.copy(out=qkT[:, T:], in_=live["qkT_ps", n][:, T:])
+                nc.scalar.copy(out=qkT[:, : T + P], in_=live["qkT_ps", n][:, : T + P])
+                nc.vector.tensor_copy(out=qkT[:, T + P :], in_=live["q_rest_ps"][:, T + P :])
             else:
                 nc.scalar.copy(out=qkT[:], in_=live["qkT_ps", n][:])
             live["qkT", n] = qkT
@@ -262,8 +271,8 @@ def tile_dualstreamattentionwithrotaryembedding_pb_t_kernel(
                 return
             n, i = divmod(k, TILES)
             qkT = live["qkT", n]
-            s_ps = ps_scores.tile([P, T], F32)
-            nc.tensor.matmul(out=s_ps[:], lhsT=qkT[:, i * P : (i + 1) * P], rhs=qkT[:, T:], start=True, stop=True)
+            s_ps = ps_scores.tile([P, T], F32, tag="s_ps")
+            nc.tensor.matmul(out=s_ps[:], lhsT=qkT[:, T + i * P : T + (i + 1) * P], rhs=qkT[:, :T], start=True, stop=True)
             live["s_ps", k] = s_ps
 
         def row_maximum(k):
@@ -347,46 +356,107 @@ def tile_dualstreamattentionwithrotaryembedding_pb_t_kernel(
             if not 0 <= n < HEADS:
                 return
             inv_sum = head.tile([P, TILES], F32)
-            nc.gpsimd.tensor_tensor(out=inv_sum[:], in0=live["rowsum", n][:], in1=minus_one[:], op=ALU.pow)
+            nc.vector.reciprocal(out=inv_sum[:], in_=live["rowsum", n][:])
             live["inv_sum", n] = inv_sum
 
         def normalise(n):
             if not 0 <= n < HEADS:
                 return
             b, h = divmod(n, H)
-            if h == 0:
-                y_sb = batch.tile([P, TILES, D], F32)
-                live["y", b] = y_sb
-            inv_sum = live["inv_sum", n]
+            if b == B - 1:
+                y_head = head.tile([P, TILES, HD], F32)
+                live["y_head", n] = y_head
+                y_out = y_head[:]
+            else:
+                if h == 0:
+                    y_sb = batch.tile([P, TILES, D], F32)
+                    live["y", b] = y_sb
+                y_out = live["y", b][:, :, h * HD : (h + 1) * HD]
             nc.vector.tensor_tensor(
-                out=live["y", b][:, :, h * HD : (h + 1) * HD],
+                out=y_out,
                 in0=live["y_ps", n][:],
-                in1=inv_sum[:].unsqueeze(2).to_broadcast([P, TILES, HD]),
+                in1=live["inv_sum", n][:].unsqueeze(2).to_broadcast([P, TILES, HD]),
                 op=ALU.mult,
             )
-            if h == H - 1:
+            if b == B - 1:
+                store_head(n)
+            elif h == H - 1:
                 store_y(b)
+
+        def last_transpose_e(i):
+            e_words = live["e", LAST * TILES + i][:].bitcast(F32)
+            eT_ps = ps_scores.tile([P, 2, HALF], F32, tag="s_ps")
+            for u in range(2):
+                nc.tensor.transpose(eT_ps[:, u, :P], e_words[:, u * P : (u + 1) * P], ident_f32[:])
+            live["last_eT_ps", i] = eT_ps
+
+        def last_copy_eT(i):
+            if i == 0:
+                e_grouped = head.tile([P, T * PACK], BF16, align_bytes=64)
+                live["e_grouped", LAST] = e_grouped
+                e_codes = head.tile([P, T], U32, align_bytes=64)
+                e_scales = head.tile([P, T], U8, align_bytes=64)
+                live["e_codes", LAST] = e_codes
+                live["e_scales", LAST] = e_scales
+            e_grouped_words = live["e_grouped", LAST][:].bitcast(F32).rearrange("p (q u) -> p q u", u=2)
+            nc.scalar.copy(
+                out=e_grouped_words[:, i * P : (i + 1) * P, :],
+                in_=live["last_eT_ps", i][:, :, :P].rearrange("p u q -> p q u"),
+            )
+
+        def last_quantise_e(i):
+            qs = slice(i * P, (i + 1) * P)
+            nc.vector.quantize_mx(
+                out=live["e_codes", LAST][:, qs].bitcast(FP8X4),
+                scales=live["e_scales", LAST][:, qs],
+                in_=live["e_grouped", LAST][:, i * P * PACK : (i + 1) * P * PACK],
+            )
+
+        def last_multiply_ev(i):
+            qs = slice(i * P, (i + 1) * P)
+            y_ps = ps_scores.tile([P, T], F32, tag="s_ps")
+            nc.tensor.matmul_mx(
+                out=y_ps[:, :HD],
+                lhsT=live["e_codes", LAST][:, qs].bitcast(FP8X4),
+                lhsT_scale=live["e_scales", LAST][:, qs],
+                rhs=live["v_codes", LAST][:].bitcast(FP8X4),
+                rhs_scale=live["v_scales", LAST][:],
+                start=True,
+                stop=True,
+            )
+            live["last_y_ps", i] = y_ps
+
+        def last_normalise(i):
+            b, h = divmod(LAST, H)
+            cols = slice(h * HD, (h + 1) * HD)
+            y_rows = rows.tile([P, HD], F32)
+            nc.vector.tensor_scalar(
+                out=y_rows[:], in0=live["last_y_ps", i][:, :HD],
+                scalar1=live["inv_sum", LAST][:, i : i + 1], scalar2=None, op0=ALU.mult,
+            )
+            if i == 0:
+                nc.sync.dma_start(out=out_1[b][:, cols], in_=y_rows[:])
+            else:
+                nc.sync.dma_start(out=out_0[b, (i - 1) * P : i * P, cols], in_=y_rows[:])
 
         transpose_qk(0)
         copy_qkT(0)
         group_w_c()
         group_w_x(0)
         group_w_x(1)
-        for n in range(-1, HEADS + 2):
+        for n in range(-1, HEADS):
             b, h = divmod(n, H)
             k = n * TILES
             if h == 0:
                 load_qk(b + 2)
                 load_x(b + 2)
-            v_heads = [m for m in range(HEADS) if max(m, V_FIRST) == n]
             first = n == 0
             xp = (n + 3) // 2 if n > 0 and n % 2 == 1 else -1
             scores(k + 3)
+            project_v(n - 1)
             transpose_e(n - 1, 1)
-            for m in v_heads:
-                project_v(m)
             row_maximum(k + 2)
-            normalise(n - 2)
+            quantise_v(n - 2)
             if first:
                 transpose_x(0)
                 quantise_w(0)
@@ -396,9 +466,10 @@ def tile_dualstreamattentionwithrotaryembedding_pb_t_kernel(
             copy_xT(xp)
             scores(k + 4)
             row_maximum(k + 3)
-            for m in v_heads:
-                add_bias_v(m)
+            invert_sums(n - 2)
+            add_bias_v(n - 1)
             if n>=0: transpose_qk(n + 2)
+            multiply_ev(n - 2)
             exponentials(k + 1)
             if first:
                 group_w_x(3)
@@ -406,29 +477,60 @@ def tile_dualstreamattentionwithrotaryembedding_pb_t_kernel(
                 transpose_x(1)
             copy_eT(n - 1, 1)
             scores(k + 5)
-            transpose_e(n, 0)
+            if n < LAST:
+                transpose_e(n, 0)
+            else:
+                last_transpose_e(0)
             row_maximum(k + 4)
-            quantise_e(n - 1)
+            normalise(n - 2)
+            quantise_x(xp)
             if first:
                 quantise_x(0)
                 quantise_w(1)
                 group_bias(0)
+            if n == LAST:
+                project_v(n)
             exponentials(k + 2)
             if n>=0: copy_qkT(n + 2)
+            if n == LAST: last_copy_eT(0)
             if first:
                 copy_xT(1)
             scores(k + 6)
+            if n == LAST:
+                last_transpose_e(1)
             if n<0: transpose_qk(n+2)
             row_maximum(k + 5)
-            for m in v_heads:
-                quantise_v(m)
             if first:
                 quantise_x(1)
-            quantise_x(xp)
+            quantise_e(n - 1)
+            if n == LAST:
+                quantise_v(n-1)
+                add_bias_v(n)
             if 0<=n<H-1:
                 group_bias(n+1)
-            multiply_ev(n - 1)
-            invert_sums(n - 1)
             if n>=0 and n%2==0: transpose_x((n + 4)//2)
             exponentials(k + 3)
-            copy_eT(n, 0)
+            if n < LAST:
+                copy_eT(n, 0)
+        last_copy_eT(1)
+        last_transpose_e(2)
+        invert_sums(LAST - 1)
+        last_quantise_e(0)
+        quantise_v(LAST)
+        multiply_ev(LAST - 1)
+        last_copy_eT(2)
+        last_transpose_e(3)
+        invert_sums(LAST)
+        last_quantise_e(1)
+        last_multiply_ev(0)
+        normalise(LAST - 1)
+        last_copy_eT(3)
+        last_multiply_ev(1)
+        last_quantise_e(2)
+        last_normalise(0)
+        last_multiply_ev(2)
+        last_quantise_e(3)
+        last_normalise(1)
+        last_multiply_ev(3)
+        last_normalise(2)
+        last_normalise(3)

@@ -52,6 +52,10 @@ def tile_dualstreamattentionwithrotaryembedding_pb_t_kernel(
         nc.gpsimd.memset(warm[:], 0.0)
         warm_exp = const.tile([P, 1], F32)
         nc.scalar.activation(out=warm_exp[:], in_=warm[:], func=ACT.Exp)
+        row_max = const.tile([P, ROW_TILES], F32)
+        shift = const.tile([P, ROW_TILES], F32)
+        rowsum = const.tile([P, ROW_TILES], F32)
+        inv_sum = const.tile([P, ROW_TILES], F32)
         ident_bf16 = const.tile([P, P], BF16)
         make_identity(nc, ident_bf16[:])
         ident_f32 = const.tile([P, P], F32)
@@ -278,29 +282,27 @@ def tile_dualstreamattentionwithrotaryembedding_pb_t_kernel(
         def row_maximum(k):
             if not 0 <= k < ROW_TILES:
                 return
-            row_max = rows.tile([P, 1], F32)
-            nc.vector.reduce_max(out=row_max[:], in_=live["s_ps", k][:], axis=mybir.AxisListType.X)
-            shift = rows.tile([P, 1], F32)
+            nc.vector.reduce_max(out=row_max[:, k : k + 1], in_=live["s_ps", k][:], axis=mybir.AxisListType.X)
             nc.gpsimd.tensor_scalar(
-                out=shift[:], in0=row_max[:], scalar1=-SCALE, scalar2=0.0, op0=ALU.mult, op1=ALU.add
+                out=shift[:, k : k + 1],
+                in0=row_max[:, k : k + 1],
+                scalar1=-SCALE,
+                scalar2=0.0,
+                op0=ALU.mult,
+                op1=ALU.add,
             )
-            live["shift", k] = shift
 
         def exponentials(k):
             if not 0 <= k < ROW_TILES:
                 return
-            n, i = divmod(k, TILES)
-            if i == 0:
-                rowsum = head.tile([P, TILES], F32)
-                live["rowsum", n] = rowsum
             e_sb = rows.tile([P, T], BF16)
             nc.scalar.activation(
                 out=e_sb[:].rearrange("q (u p e) -> q u p e", u=2, e=2),
                 in_=live["s_ps", k][:].rearrange("q (u e p) -> q u p e", u=2, e=2),
                 func=ACT.Exp,
-                bias=live["shift", k][:],
+                bias=shift[:, k : k + 1],
                 scale=SCALE,
-                accum_out=live["rowsum", n][:, i : i + 1],
+                accum_out=rowsum[:, k : k + 1],
             )
             live["e", k] = e_sb
 
@@ -355,9 +357,8 @@ def tile_dualstreamattentionwithrotaryembedding_pb_t_kernel(
         def invert_sums(n):
             if not 0 <= n < HEADS:
                 return
-            inv_sum = head.tile([P, TILES], F32)
-            nc.vector.reciprocal(out=inv_sum[:], in_=live["rowsum", n][:])
-            live["inv_sum", n] = inv_sum
+            ks = slice(n * TILES, (n + 2) * TILES)
+            nc.vector.reciprocal(out=inv_sum[:, ks], in_=rowsum[:, ks])
 
         def normalise(n):
             if not 0 <= n < HEADS:
@@ -375,7 +376,7 @@ def tile_dualstreamattentionwithrotaryembedding_pb_t_kernel(
             nc.vector.tensor_tensor(
                 out=y_out,
                 in0=live["y_ps", n][:],
-                in1=live["inv_sum", n][:].unsqueeze(2).to_broadcast([P, TILES, HD]),
+                in1=inv_sum[:, n * TILES : (n + 1) * TILES].unsqueeze(2).to_broadcast([P, TILES, HD]),
                 op=ALU.mult,
             )
             if b == B - 1:
@@ -432,7 +433,7 @@ def tile_dualstreamattentionwithrotaryembedding_pb_t_kernel(
             y_rows = rows.tile([P, HD], F32)
             nc.vector.tensor_scalar(
                 out=y_rows[:], in0=live["last_y_ps", i][:, :HD],
-                scalar1=live["inv_sum", LAST][:, i : i + 1], scalar2=None, op0=ALU.mult,
+                scalar1=inv_sum[:, LAST * TILES + i : LAST * TILES + i + 1], scalar2=None, op0=ALU.mult,
             )
             if i == 0:
                 nc.sync.dma_start(out=out_1[b][:, cols], in_=y_rows[:])
@@ -466,7 +467,8 @@ def tile_dualstreamattentionwithrotaryembedding_pb_t_kernel(
             copy_xT(xp)
             scores(k + 4)
             row_maximum(k + 3)
-            invert_sums(n - 2)
+            if n % 2 == 0:
+                invert_sums(n - 2)
             add_bias_v(n - 1)
             if n>=0: transpose_qk(n + 2)
             multiply_ev(n - 2)
@@ -514,13 +516,12 @@ def tile_dualstreamattentionwithrotaryembedding_pb_t_kernel(
                 copy_eT(n, 0)
         last_copy_eT(1)
         last_transpose_e(2)
-        invert_sums(LAST - 1)
         last_quantise_e(0)
         quantise_v(LAST)
         multiply_ev(LAST - 1)
         last_copy_eT(2)
         last_transpose_e(3)
-        invert_sums(LAST)
+        invert_sums(LAST - 1)
         last_quantise_e(1)
         last_multiply_ev(0)
         normalise(LAST - 1)

@@ -153,8 +153,8 @@ def tile_dualstreamattentionwithrotaryembedding_pb_t_kernel(
                 scalar1=1.0, scalar2=0.0, op0=ALU.mult, op1=ALU.add,
             )
 
-        load_qk(1)
         load_x(1)
+        load_qk(1)
 
         def transpose_x(xp):
             if not 0 <= xp < 2 * B:
@@ -442,9 +442,6 @@ def tile_dualstreamattentionwithrotaryembedding_pb_t_kernel(
 
         transpose_qk(0)
         copy_qkT(0)
-        group_w_c()
-        group_w_x(0)
-        group_w_x(1)
         for n in range(-1, HEADS):
             b, h = divmod(n, H)
             k = n * TILES
@@ -460,7 +457,7 @@ def tile_dualstreamattentionwithrotaryembedding_pb_t_kernel(
             quantise_v(n - 2)
             if first:
                 transpose_x(0)
-                quantise_w(0)
+                group_w_c()
                 group_w_x(2)
             exponentials(k)
             if first: copy_qkT(1)
@@ -475,6 +472,7 @@ def tile_dualstreamattentionwithrotaryembedding_pb_t_kernel(
             exponentials(k + 1)
             if first:
                 group_w_x(3)
+                quantise_w(0)
                 copy_xT(0)
                 transpose_x(1)
             copy_eT(n - 1, 1)
@@ -484,6 +482,8 @@ def tile_dualstreamattentionwithrotaryembedding_pb_t_kernel(
             else:
                 last_transpose_e(0)
             row_maximum(k + 4)
+            if n < 0:
+                group_w_x(0)
             normalise(n - 2)
             quantise_x(xp)
             if first:
@@ -502,6 +502,8 @@ def tile_dualstreamattentionwithrotaryembedding_pb_t_kernel(
                 last_transpose_e(1)
             if n<0: transpose_qk(n+2)
             row_maximum(k + 5)
+            if n < 0:
+                group_w_x(1)
             if first:
                 quantise_x(1)
             quantise_e(n - 1)

@@ -40,9 +40,8 @@ def tile_dualstreamattentionwithrotaryembedding_pb_t_kernel(
         head = ctx.enter_context(tc.tile_pool(name="head", bufs=4))
         rows = ctx.enter_context(tc.tile_pool(name="rows", bufs=6))
         ahead = ctx.enter_context(tc.tile_pool(name="ahead", bufs=6))
-        ps_scores = ctx.enter_context(tc.psum_pool(name="ps_scores", bufs=4))
+        ps_scores = ctx.enter_context(tc.psum_pool(name="ps_scores", bufs=5))
         ps_eT = ctx.enter_context(tc.psum_pool(name="ps_eT", bufs=1))
-        ps_y = ctx.enter_context(tc.psum_pool(name="ps_y", bufs=1))
         ps_misc = ctx.enter_context(tc.psum_pool(name="ps_misc", bufs=2))
         ctx.enter_context(tc.manual_schedule())
 
@@ -340,7 +339,7 @@ def tile_dualstreamattentionwithrotaryembedding_pb_t_kernel(
         def multiply_ev(n):
             if not 0 <= n < HEADS:
                 return
-            y_ps = ps_y.tile([P, TILES, HD], F32)
+            y_ps = ps_misc.tile([P, TILES, HD], F32, tag="misc")
             for i in range(TILES):
                 qs = slice(i * P, (i + 1) * P)
                 nc.tensor.matmul_mx(
@@ -450,10 +449,11 @@ def tile_dualstreamattentionwithrotaryembedding_pb_t_kernel(
                 load_x(b + 2)
             first = n == 0
             xp = (n + 3) // 2 if n > 0 and n % 2 == 1 else -1
-            scores(k + 3)
+            if not first:
+                scores(k + 4)
             project_v(n - 1)
             transpose_e(n - 1, 1)
-            row_maximum(k + 2)
+            row_maximum(k + 3)
             quantise_v(n - 2)
             if first:
                 transpose_x(0)
@@ -462,13 +462,14 @@ def tile_dualstreamattentionwithrotaryembedding_pb_t_kernel(
             exponentials(k)
             if first: copy_qkT(1)
             copy_xT(xp)
-            scores(k + 4)
-            row_maximum(k + 3)
+            if first:
+                scores(k + 4)
+            scores(k + 5)
+            row_maximum(k + 4)
             if n % 2 == 0:
                 invert_sums(n - 2)
             add_bias_v(n - 1)
             if n>=0: transpose_qk(n + 2)
-            multiply_ev(n - 2)
             exponentials(k + 1)
             if first:
                 group_w_x(3)
@@ -476,15 +477,16 @@ def tile_dualstreamattentionwithrotaryembedding_pb_t_kernel(
                 copy_xT(0)
                 transpose_x(1)
             copy_eT(n - 1, 1)
-            scores(k + 5)
+            scores(k + 6)
             if n < LAST:
                 transpose_e(n, 0)
             else:
                 last_transpose_e(0)
-            row_maximum(k + 4)
+            row_maximum(k + 5)
             if n < 0:
                 group_w_x(0)
-            normalise(n - 2)
+            multiply_ev(n - 2)
+            quantise_e(n - 1)
             quantise_x(xp)
             if first:
                 quantise_x(0)
@@ -497,16 +499,16 @@ def tile_dualstreamattentionwithrotaryembedding_pb_t_kernel(
             if n == LAST: last_copy_eT(0)
             if first:
                 copy_xT(1)
-            scores(k + 6)
+            scores(k + 7)
             if n == LAST:
                 last_transpose_e(1)
             if n<0: transpose_qk(n+2)
-            row_maximum(k + 5)
+            row_maximum(k + 6)
             if n < 0:
                 group_w_x(1)
             if first:
                 quantise_x(1)
-            quantise_e(n - 1)
+            normalise(n - 2)
             if n == LAST:
                 quantise_v(n-1)
                 add_bias_v(n)

import math
from contextlib import ExitStack

import concourse.mybir as mybir
from concourse.masks import make_identity

BF16 = mybir.dt.bfloat16
F32 = mybir.dt.float32
U32 = mybir.dt.uint32
U8 = mybir.dt.uint8
FP8X4 = mybir.dt.float8_e4m3fn_x4
ALU = mybir.AluOpType
ACT = mybir.ActivationFunctionType

B = 12
H = 4
T = 512
D = 512
HD = 128
P = 128
PACK = 4
TILES = T // P
HALF = 2 * P
SCALE = 1.0 / math.sqrt(HD)
LAST = B * H - 1
HEADS = B * H
ROW_TILES = HEADS * TILES

FLOPS = 2 * B * T * D * D + 2 * 2 * B * H * T * T * HD


def tile_dualstreamattentionwithrotaryembedding_pb_t_kernel(
    tc, q_rot, k_rot, x, c, Wv_x, bv_x, Wv_c, bv_c, out_0, out_1
):
    nc = tc.nc
    with ExitStack() as ctx:
        const = ctx.enter_context(tc.tile_pool(name="const", bufs=1))
        loads = ctx.enter_context(tc.tile_pool(name="loads", bufs=3))
        batch = ctx.enter_context(tc.tile_pool(name="batch", bufs=2))
        head = ctx.enter_context(tc.tile_pool(name="head", bufs=4))
        rows = ctx.enter_context(tc.tile_pool(name="rows", bufs=6))
        ahead = ctx.enter_context(tc.tile_pool(name="ahead", bufs=6))
        ps_scores = ctx.enter_context(tc.psum_pool(name="ps_scores", bufs=5))
        ps_eT = ctx.enter_context(tc.psum_pool(name="ps_eT", bufs=1))
        ps_misc = ctx.enter_context(tc.psum_pool(name="ps_misc", bufs=2))
        ctx.enter_context(tc.manual_schedule())

        live = {}

        warm = const.tile([P, 1], F32)
        nc.gpsimd.memset(warm[:], 0.0)
        warm_exp = const.tile([P, 1], F32)
        nc.scalar.activation(out=warm_exp[:], in_=warm[:], func=ACT.Exp)
        row_max = const.tile([P, ROW_TILES], F32)
        shift = const.tile([P, ROW_TILES], F32)
        rowsum = const.tile([P, ROW_TILES], F32)
        inv_sum = const.tile([P, ROW_TILES], F32)
        ident_bf16 = const.tile([P, P], BF16)
        make_identity(nc, ident_bf16[:])
        ident_f32 = const.tile([P, P], F32)
        make_identity(nc, ident_f32[:])

        def load_x(b):
            if not 0 <= b < B:
                return
            xc_sb = loads.tile([P, TILES * D], BF16)
            nc.sync.dma_start(out=xc_sb[:, 0:D], in_=c[b])
            nc.sync.dma_start(
                out=xc_sb[:, D:].rearrange("p (t k) -> p t k", k=D),
                in_=x[b].rearrange("(t p) k -> p t k", p=P),
            )
            live["xc", b] = xc_sb

        def load_qk(b):
            if not 0 <= b < B:
                return
            q_sb = loads.tile([P, H * TILES, HD], BF16)
            k_sb = loads.tile([P, H * TILES, HD], BF16)
            live["q", b] = q_sb
            live["k", b] = k_sb
            load_qk_heads(b, 0, 1 if b == 0 else H)

        def load_qk_heads(b, first, last):
            for name, src in (("k", k_rot), ("q", q_rot)):
                nc.sync.dma_start(
                    out=live[name, b][:, first * TILES : last * TILES, :],
                    in_=src[b, first:last].rearrange("h (t p) d -> p (h t) d", p=P),
                )

        def store_head(n):
            b, h = divmod(n, H)
            cols = slice(h * HD, (h + 1) * HD)
            y_head = live["y_head", n]
            nc.sync.dma_start(out=out_0[b].rearrange("(t p) n -> p t n", p=P)[:, :, cols], in_=y_head[:, 1:, :])
            nc.sync.dma_start(out=out_1[b][:, cols], in_=y_head[:, 0, :])

        def store_y(b):
            if not 0 <= b < B:
                return
            y_sb = live["y", b]
            nc.sync.dma_start(out=out_1[b], in_=y_sb[:, 0, :])
            nc.sync.dma_start(out=out_0[b].rearrange("(t p) n -> p t n", p=P), in_=y_sb[:, 1:, :])

        load_qk(0)
        w_codes = const.tile([P, 2, D], U32, align_bytes=64)
        w_scales = const.tile([P, 2, D], U8, align_bytes=64)
        w_rows = const.tile([P, 2, PACK * D], BF16)
        for stream, w in enumerate((Wv_c, Wv_x)):
            nc.sync.dma_start(
                out=w_rows[:, stream, :].rearrange("p (u m) -> p u m", u=2),
                in_=w.rearrange("(u p e) n -> p u (e n)", u=2, e=2),
            )
        load_qk_heads(0, 1, 2)
        load_x(0)
        load_qk_heads(0, 2, H)
        bias_rows = const.tile([P, 2, D], BF16)
        nc.sync.dma_start(out=bias_rows[:, 0, :], in_=bv_c.partition_broadcast(P))
        nc.sync.dma_start(out=bias_rows[:, 1, :], in_=bv_x.partition_broadcast(P))
        w_grouped = const.tile([P, 2, D * PACK], BF16, align_bytes=64)

        def group_w_c():
            nc.vector.tensor_copy(
                out=w_grouped[:, 0, :].rearrange("p (n t) -> p n t", t=PACK),
                in_=w_rows[:, 0, :].rearrange("p (t n) -> p n t", t=PACK),
            )

        def group_w_x(h):
            cols = slice(h * HD, (h + 1) * HD)
            nc.gpsimd.tensor_scalar(
                out=w_grouped[:, 1, :].rearrange("p (n t) -> p n t", t=PACK)[:, cols, :],
                in0=w_rows[:, 1, :].rearrange("p (t n) -> p n t", t=PACK)[:, cols, :],
                scalar1=1.0, scalar2=0.0, op0=ALU.mult, op1=ALU.add,
            )

        def quantise_w(stream):
            nc.vector.quantize_mx(
                out=w_codes[:, stream, :].bitcast(FP8X4), scales=w_scales[:, stream, :], in_=w_grouped[:, stream, :]
            )

        bias_grouped = const.tile([P, D, PACK], F32)

        def group_bias(h):
            cols = slice(h * HD, (h + 1) * HD)
            nc.gpsimd.tensor_scalar(
                out=bias_grouped[:, cols, :],
                in0=bias_rows[:, 1, cols].unsqueeze(2).to_broadcast([P, HD, PACK]),
                scalar1=1.0, scalar2=0.0, op0=ALU.mult, op1=ALU.add,
            )
            nc.gpsimd.tensor_scalar(
                out=bias_grouped[:, cols, 0],
                in0=bias_rows[:, 0, cols],
                scalar1=1.0, scalar2=0.0, op0=ALU.mult, op1=ALU.add,
            )

        load_x(1)
        load_qk(1)

        def transpose_x(xp):
            if not 0 <= xp < 2 * B:
                return
            b, pair = divmod(xp, 2)
            xc_words = live["xc", b][:].bitcast(F32)
            xT_ps = ps_misc.tile([P, 2, HALF], F32, tag="misc")
            for j in range(2):
                for u in range(2):
                    first = (2 * pair + j) * (D // 2) + u * P
                    nc.tensor.transpose(
                        xT_ps[:, u, j * P : (j + 1) * P], xc_words[:, first : first + P], ident_f32[:]
                    )
            live["xT_ps", xp] = xT_ps

        def copy_xT(xp):
            if not 0 <= xp < 2 * B:
                return
            x_grouped = head.tile([P, HALF * PACK], BF16, align_bytes=64)
            nc.scalar.copy(
                out=x_grouped[:].bitcast(F32).rearrange("p (s u) -> p s u", u=2),
                in_=live["xT_ps", xp][:].rearrange("p u s -> p s u"),
            )
            live["x_grouped", xp] = x_grouped

        def quantise_x(xp):
            if not 0 <= xp < 2 * B:
                return
            b, pair = divmod(xp, 2)
            if pair == 0:
                x_codes = batch.tile([P, T], U32, align_bytes=64)
                x_scales = batch.tile([P, T], U8, align_bytes=64)
                live["x_codes", b] = x_codes
                live["x_scales", b] = x_scales
            toks = slice(pair * HALF, (pair + 1) * HALF)
            nc.vector.quantize_mx(
                out=live["x_codes", b][:, toks].bitcast(FP8X4),
                scales=live["x_scales", b][:, toks],
                in_=live["x_grouped", xp][:],
            )

        def project_v(n):
            if not 0 <= n < HEADS:
                return
            b, h = divmod(n, H)
            cols = slice(h * HD, (h + 1) * HD)
            v_ps = ps_misc.tile([P, TILES, HD], F32, tag="misc")
            for t in range(TILES):
                stream = 0 if t == 0 else 1
                toks = slice(t * P, (t + 1) * P)
                nc.tensor.matmul_mx(
                    out=v_ps[:, t, :],
                    lhsT=live["x_codes", b][:, toks].bitcast(FP8X4),
                    lhsT_scale=live["x_scales", b][:, toks],
                    rhs=w_codes[:, stream, cols].bitcast(FP8X4),
                    rhs_scale=w_scales[:, stream, cols],
                    start=True,
                    stop=True,
                )
            live["v_ps", n] = v_ps

        def add_bias_v(n):
            if not 0 <= n < HEADS:
                return
            h = n % H
            v_grouped = head.tile([P, HD, PACK], BF16, align_bytes=64)
            nc.vector.tensor_tensor(
                out=v_grouped[:],
                in0=live["v_ps", n][:].rearrange("p t d -> p d t"),
                in1=bias_grouped[:, h * HD : (h + 1) * HD, :],
                op=ALU.add,
            )
            live["v_grouped", n] = v_grouped

        def quantise_v(n):
            if not 0 <= n < HEADS:
                return
            v_codes = ahead.tile([P, HD], U32, align_bytes=64)
            v_scales = ahead.tile([P, HD], U8, align_bytes=64)
            nc.vector.quantize_mx(
                out=v_codes[:].bitcast(FP8X4),
                scales=v_scales[:],
                in_=live["v_grouped", n][:].rearrange("p d t -> p (d t)"),
            )
            live["v_codes", n] = v_codes
            live["v_scales", n] = v_scales

        def transpose_qk(n):
            if not 0 <= n < HEADS:
                return
            b, h = divmod(n, H)
            qkT_ps = ps_misc.tile([P, 2 * T], BF16, tag="misc")
            live["qkT_ps", n] = qkT_ps
            for t in range(TILES):
                nc.tensor.transpose(qkT_ps[:, t * P : (t + 1) * P], live["k", b][:, h * TILES + t, :], ident_bf16[:])
            if n == 0:
                qkT_ps = ps_misc.tile([P, 2 * T], BF16, tag="misc")
                live["q_rest_ps"] = qkT_ps
            for t in range(TILES):
                bank = live["qkT_ps", n] if t == 0 else qkT_ps
                nc.tensor.transpose(
                    bank[:, T + t * P : T + (t + 1) * P], live["q", b][:, h * TILES + t, :], ident_bf16[:]
                )

        def copy_qkT(n):
            if not 0 <= n < HEADS:
                return
            qkT = head.tile([P, 2 * T], BF16)
            if n == 0:
                nc.scalar.copy(out=qkT[:, : T + P], in_=live["qkT_ps", n][:, : T + P])
                nc.vector.tensor_copy(out=qkT[:, T + P :], in_=live["q_rest_ps"][:, T + P :])
            else:
                nc.scalar.copy(out=qkT[:], in_=live["qkT_ps", n][:])
            live["qkT", n] = qkT

        def scores(k):
            if not 0 <= k < ROW_TILES:
                return
            n, i = divmod(k, TILES)
            qkT = live["qkT", n]
            s_ps = ps_scores.tile([P, T], F32, tag="s_ps")
            nc.tensor.matmul(out=s_ps[:], lhsT=qkT[:, T + i * P : T + (i + 1) * P], rhs=qkT[:, :T], start=True, stop=True)
            live["s_ps", k] = s_ps

        def row_maximum(k):
            if not 0 <= k < ROW_TILES:
                return
            nc.vector.reduce_max(out=row_max[:, k : k + 1], in_=live["s_ps", k][:], axis=mybir.AxisListType.X)
            nc.gpsimd.tensor_scalar(
                out=shift[:, k : k + 1],
                in0=row_max[:, k : k + 1],
                scalar1=-SCALE,
                scalar2=0.0,
                op0=ALU.mult,
                op1=ALU.add,
            )

        def exponentials(k):
            if not 0 <= k < ROW_TILES:
                return
            e_sb = rows.tile([P, T], BF16)
            nc.scalar.activation(
                out=e_sb[:].rearrange("q (u p e) -> q u p e", u=2, e=2),
                in_=live["s_ps", k][:].rearrange("q (u e p) -> q u p e", u=2, e=2),
                func=ACT.Exp,
                bias=shift[:, k : k + 1],
                scale=SCALE,
                accum_out=rowsum[:, k : k + 1],
            )
            live["e", k] = e_sb

        def transpose_e(n, pair):
            if not 0 <= n < HEADS:
                return
            eT_ps = ps_eT.tile([P, 2, HALF], F32)
            for j in range(2):
                e_words = live["e", n * TILES + 2 * pair + j][:].bitcast(F32)
                for u in range(2):
                    nc.tensor.transpose(eT_ps[:, u, j * P : (j + 1) * P], e_words[:, u * P : (u + 1) * P], ident_f32[:])
            live["eT_ps", n, pair] = eT_ps

        def copy_eT(n, pair):
            if not 0 <= n < HEADS:
                return
            if pair == 0:
                e_grouped = head.tile([P, T * PACK], BF16, align_bytes=64)
                live["e_grouped", n] = e_grouped
            e_grouped_words = live["e_grouped", n][:].bitcast(F32).rearrange("p (q u) -> p q u", u=2)
            nc.scalar.copy(
                out=e_grouped_words[:, pair * HALF : (pair + 1) * HALF, :],
                in_=live["eT_ps", n, pair][:].rearrange("p u q -> p q u"),
            )

        def quantise_e(n):
            if not 0 <= n < HEADS:
                return
            e_codes = head.tile([P, T], U32, align_bytes=64)
            e_scales = head.tile([P, T], U8, align_bytes=64)
            nc.vector.quantize_mx(out=e_codes[:].bitcast(FP8X4), scales=e_scales[:], in_=live["e_grouped", n][:])
            live["e_codes", n] = e_codes
            live["e_scales", n] = e_scales

        def multiply_ev(n):
            if not 0 <= n < HEADS:
                return
            y_ps = ps_misc.tile([P, TILES, HD], F32, tag="misc")
            for i in range(TILES):
                qs = slice(i * P, (i + 1) * P)
                nc.tensor.matmul_mx(
                    out=y_ps[:, i, :],
                    lhsT=live["e_codes", n][:, qs].bitcast(FP8X4),
                    lhsT_scale=live["e_scales", n][:, qs],
                    rhs=live["v_codes", n][:].bitcast(FP8X4),
                    rhs_scale=live["v_scales", n][:],
                    start=True,
                    stop=True,
                )
            live["y_ps", n] = y_ps

        def invert_sums(n):
            if not 0 <= n < HEADS:
                return
            ks = slice(n * TILES, (n + 2) * TILES)
            nc.vector.reciprocal(out=inv_sum[:, ks], in_=rowsum[:, ks])

        def normalise(n):
            if not 0 <= n < HEADS:
                return
            b, h = divmod(n, H)
            if b == B - 1:
                y_head = head.tile([P, TILES, HD], F32)
                live["y_head", n] = y_head
                y_out = y_head[:]
            else:
                if h == 0:
                    y_sb = batch.tile([P, TILES, D], F32)
                    live["y", b] = y_sb
                y_out = live["y", b][:, :, h * HD : (h + 1) * HD]
            nc.vector.tensor_tensor(
                out=y_out,
                in0=live["y_ps", n][:],
                in1=inv_sum[:, n * TILES : (n + 1) * TILES].unsqueeze(2).to_broadcast([P, TILES, HD]),
                op=ALU.mult,
            )
            if b == B - 1:
                store_head(n)
            elif h == H - 1:
                store_y(b)

        def last_transpose_e(i):
            e_words = live["e", LAST * TILES + i][:].bitcast(F32)
            eT_ps = ps_scores.tile([P, 2, HALF], F32, tag="s_ps")
            for u in range(2):
                nc.tensor.transpose(eT_ps[:, u, :P], e_words[:, u * P : (u + 1) * P], ident_f32[:])
            live["last_eT_ps", i] = eT_ps

        def last_copy_eT(i):
            if i == 0:
                e_grouped = head.tile([P, T * PACK], BF16, align_bytes=64)
                live["e_grouped", LAST] = e_grouped
                e_codes = head.tile([P, T], U32, align_bytes=64)
                e_scales = head.tile([P, T], U8, align_bytes=64)
                live["e_codes", LAST] = e_codes
                live["e_scales", LAST] = e_scales
            e_grouped_words = live["e_grouped", LAST][:].bitcast(F32).rearrange("p (q u) -> p q u", u=2)
            nc.scalar.copy(
                out=e_grouped_words[:, i * P : (i + 1) * P, :],
                in_=live["last_eT_ps", i][:, :, :P].rearrange("p u q -> p q u"),
            )

        def last_quantise_e(i):
            qs = slice(i * P, (i + 1) * P)
            nc.vector.quantize_mx(
                out=live["e_codes", LAST][:, qs].bitcast(FP8X4),
                scales=live["e_scales", LAST][:, qs],
                in_=live["e_grouped", LAST][:, i * P * PACK : (i + 1) * P * PACK],
            )

        def last_multiply_ev(i):
            qs = slice(i * P, (i + 1) * P)
            y_ps = ps_scores.tile([P, T], F32, tag="s_ps")
            nc.tensor.matmul_mx(
                out=y_ps[:, :HD],
                lhsT=live["e_codes", LAST][:, qs].bitcast(FP8X4),
                lhsT_scale=live["e_scales", LAST][:, qs],
                rhs=live["v_codes", LAST][:].bitcast(FP8X4),
                rhs_scale=live["v_scales", LAST][:],
                start=True,
                stop=True,
            )
            live["last_y_ps", i] = y_ps

        def last_normalise(i):
            b, h = divmod(LAST, H)
            cols = slice(h * HD, (h + 1) * HD)
            y_rows = rows.tile([P, HD], F32)
            nc.vector.tensor_scalar(
                out=y_rows[:], in0=live["last_y_ps", i][:, :HD],
                scalar1=inv_sum[:, LAST * TILES + i : LAST * TILES + i + 1], scalar2=None, op0=ALU.mult,
            )
            if i == 0:
                nc.sync.dma_start(out=out_1[b][:, cols], in_=y_rows[:])
            else:
                nc.sync.dma_start(out=out_0[b, (i - 1) * P : i * P, cols], in_=y_rows[:])

        transpose_qk(0)
        copy_qkT(0)
        for n in range(-1, HEADS):
            b, h = divmod(n, H)
            k = n * TILES
            if h == 0:
                load_qk(b + 2)
                load_x(b + 2)
            first = n == 0
            xp = (n + 3) // 2 if n > 0 and n % 2 == 1 else -1
            if not first:
                scores(k + 4)
            project_v(n - 1)
            transpose_e(n - 1, 1)
            row_maximum(k + 3)
            quantise_v(n - 2)
            if first:
                transpose_x(0)
                group_w_c()
                group_w_x(2)
            exponentials(k)
            if first: copy_qkT(1)
            copy_xT(xp)
            if first:
                scores(k + 4)
            scores(k + 5)
            row_maximum(k + 4)
            if n % 2 == 0:
                invert_sums(n - 2)
            add_bias_v(n - 1)
            if n>=0: transpose_qk(n + 2)
            exponentials(k + 1)
            if first:
                group_w_x(3)
                quantise_w(0)
                copy_xT(0)
                transpose_x(1)
            copy_eT(n - 1, 1)
            scores(k + 6)
            if n < LAST:
                transpose_e(n, 0)
            else:
                last_transpose_e(0)
            row_maximum(k + 5)
            if n < 0:
                group_w_x(0)
            multiply_ev(n - 2)
            quantise_e(n - 1)
            quantise_x(xp)
            if first:
                quantise_x(0)
                quantise_w(1)
                group_bias(0)
            if n == LAST:
                project_v(n)
            exponentials(k + 2)
            if n>=0: copy_qkT(n + 2)
            if n == LAST: last_copy_eT(0)
            if first:
                copy_xT(1)
            scores(k + 7)
            if n == LAST:
                last_transpose_e(1)
            if n<0: transpose_qk(n+2)
            row_maximum(k + 6)
            if n < 0:
                group_w_x(1)
            if first:
                quantise_x(1)
            normalise(n - 2)
            if n == LAST:
                quantise_v(n-1)
                add_bias_v(n)
            if 0<=n<H-1:
                group_bias(n+1)
            if n>=0 and n%2==0: transpose_x((n + 4)//2)
            exponentials(k + 3)
            if n < LAST:
                copy_eT(n, 0)
        last_copy_eT(1)
        last_transpose_e(2)
        last_quantise_e(0)
        quantise_v(LAST)
        multiply_ev(LAST - 1)
        last_copy_eT(2)
        last_transpose_e(3)
        invert_sums(LAST - 1)
        last_quantise_e(1)
        last_multiply_ev(0)
        normalise(LAST - 1)
        last_copy_eT(3)
        last_multiply_ev(1)
        last_quantise_e(2)
        last_normalise(0)
        last_multiply_ev(2)
        last_quantise_e(3)
        last_normalise(1)
        last_multiply_ev(3)
        last_normalise(2)
        last_normalise(3)
